import numpy as np
import ml_dtypes


def mxq(x, axis, fmt="e4m3"):
    dtype, down = {"e4m3": (ml_dtypes.float8_e4m3fn, 7), "e5m2": (ml_dtypes.float8_e5m2, 14)}[fmt]
    v = np.moveaxis(np.asarray(x, np.float32).astype(ml_dtypes.bfloat16).astype(np.float64), axis, -1)
    blocks = v.reshape(v.shape[:-1] + (-1, 32))
    amax = np.abs(blocks).max(-1, keepdims=True)
    byte = np.maximum(np.where(amax > 0, np.frexp(amax)[1] - 1 + 127, 0) - down, 1)
    scale = np.exp2(byte - 127.0)
    codes = (blocks / scale).astype(np.float32).astype(dtype).astype(np.float64)
    return np.moveaxis((codes * scale).reshape(v.shape), -1, axis)


WIDE = False


def mx_kscale(k):
    if not WIDE:
        return np.ones(k)
    levels = np.array([10, -10, 5, -5, 0])
    a = np.random.permutation(np.resize(levels, k // 512 * 4)).reshape(k // 512, 4)
    idx = np.arange(k)
    return np.exp2(a[idx // 512, idx % 128 // 32])


BF16 = ml_dtypes.bfloat16


def bf(x):
    return np.asarray(x, np.float32).astype(BF16)


def f64(x):
    return np.asarray(x).astype(np.float64)


B, I, H = 8192, 512, 128
MXK = 16 * 32


def sigmoid(v):
    return 1.0 / (1.0 + np.exp(-v))


def lin(a, w):
    if a.shape[1] % MXK == 0:
        return mxq(a, 1, "e4m3") @ mxq(w, 1, "e4m3").T
    return a @ w.T


def setup_inputs():
    s = mx_kscale(I)
    t = mx_kscale(H) if H % MXK == 0 else np.ones(H)
    inp = {"incoming": bf(np.random.standard_normal((B, I)) * s),
           "old_h": bf(np.random.standard_normal((B, H)) * t),
           "old_c": bf(np.random.standard_normal((B, H)))}
    for n in ("i", "o", "f", "c"):
        inp["w_" + n] = bf(np.random.standard_normal((H, I)) / np.sqrt(I) / s)
        inp["b_" + n] = bf(np.random.standard_normal(H) * 0.5)
        inp["u_" + n] = bf(np.random.standard_normal((H, H)) / np.sqrt(H) / t)
    return inp


def reference(incoming, old_h, old_c, w_i, b_i, u_i, w_o, b_o, u_o, w_f, b_f, u_f, w_c, b_c, u_c):
    W = np.concatenate([f64(w_i), f64(w_o), f64(w_f), f64(w_c)], axis=0)
    U = np.concatenate([f64(u_i), f64(u_o), f64(u_f), f64(u_c)], axis=0)
    b = np.concatenate([f64(b_i), f64(b_o), f64(b_f), f64(b_c)], axis=0)
    gates = lin(f64(incoming), W) + lin(f64(old_h), U) + b
    gi, go, gf, gc = np.split(gates, 4, axis=-1)
    i = sigmoid(gi)
    o = sigmoid(go)
    f = sigmoid(gf)
    c_tilde = np.tanh(gc)
    new_c = f * f64(old_c) + i * c_tilde
    new_h = o * np.tanh(new_c)
    return (new_h, new_c)

@@ -1,0 +1,235 @@
+from contextlib import ExitStack
+
+import concourse.mybir as mybir
+from concourse.masks import make_identity
+
+F32 = mybir.dt.float32
+BF16 = mybir.dt.bfloat16
+U32 = mybir.dt.uint32
+U8 = mybir.dt.uint8
+FP8X4 = mybir.dt.float8_e4m3fn_x4
+ACT = mybir.ActivationFunctionType
+ALU = mybir.AluOpType
+
+P = 128
+BATCH = 8192
+IN_F = 512
+HID = 128
+NT = BATCH // P
+GT = 4
+NG = NT // GT
+HC = 4
+GW = GT * P
+
+FLOPS = 2 * BATCH * (IN_F + HID) * 4 * HID
+
+
+def tile_lstmcell_t_kernel(
+    tc, incoming, old_h, old_c, w_i, b_i, u_i, w_o, b_o, u_o, w_f, b_f, u_f, w_c, b_c, u_c, out_0, out_1
+):
+    nc = tc.nc
+    gate_w = [w_i, w_f, w_o, w_c]
+    gate_u = [u_i, u_f, u_o, u_c]
+    gate_b = [b_i, b_f, b_o, b_c]
+
+    x_rows = incoming.rearrange("(p t) k -> p (t k)", t=NT)
+    h_rows = old_h.rearrange("(p t) k -> p (t k)", t=NT)
+    c_rows = old_c.rearrange("(p t) k -> p (t k)", t=NT)
+    nh_rows = out_0.rearrange("(p t) k -> p (t k)", t=NT)
+    ncell_rows = out_1.rearrange("(p t) k -> p (t k)", t=NT)
+
+    with ExitStack() as ctx:
+        const = ctx.enter_context(tc.tile_pool(name="const", bufs=1))
+        resident = ctx.enter_context(tc.tile_pool(name="resident", bufs=1))
+        work2 = ctx.enter_context(tc.tile_pool(name="work2", bufs=2))
+        work3 = ctx.enter_context(tc.tile_pool(name="work3", bufs=3))
+        work4 = ctx.enter_context(tc.tile_pool(name="work4", bufs=4))
+        ps_t = ctx.enter_context(tc.psum_pool(name="ps_t", bufs=3))
+        ps_mx = ctx.enter_context(tc.psum_pool(name="ps_mx", bufs=3))
+        ps_g = ctx.enter_context(tc.psum_pool(name="ps_g", bufs=2))
+
+        w_sb = const.tile([P, 4 * IN_F], BF16, name="w_sb")
+        for n in range(4):
+            nc.sync.dma_start(out=w_sb[:, n * IN_F : (n + 1) * IN_F], in_=gate_w[n])
+        u_sb = const.tile([P, 4 * HID], BF16, name="u_sb")
+        for n in range(4):
+            nc.scalar.dma_start(out=u_sb[:, n * HID : (n + 1) * HID], in_=gate_u[n])
+        b_rows = const.tile([P, P], BF16, name="b_rows")
+        nc.vector.memset(b_rows[:], 0.0)
+        for n in range(4):
+            nc.scalar.dma_start(out=b_rows[n : n + 1, :], in_=gate_b[n].rearrange("(o h) -> o h", o=1))
+
+        x_sb = []
+        h_sb = []
+        c_sb = []
+        for j in range(NG):
+            x_t = resident.tile([P, GT * IN_F], BF16, name="x%d" % j)
+            nc.sync.dma_start(out=x_t[:], in_=x_rows[:, j * GT * IN_F : (j + 1) * GT * IN_F])
+            x_sb.append(x_t)
+            if j % HC == 0:
+                m = j // HC
+                h_t = resident.tile([P, HC * GW], BF16, name="h%d" % m)
+                nc.sync.dma_start(out=h_t[:], in_=h_rows[:, m * HC * GW : (m + 1) * HC * GW])
+                h_sb.append(h_t)
+            if j % HC == 1:
+                m = j // HC
+                c_t = resident.tile([P, HC * GW], BF16, name="c%d" % m)
+                nc.sync.dma_start(out=c_t[:], in_=c_rows[:, m * HC * GW : (m + 1) * HC * GW])
+                c_sb.append(c_t)
+
+        ident_f = const.tile([P, P], F32, name="ident_f")
+        make_identity(nc, ident_f[:])
+        ident_b = const.tile([P, P], BF16, name="ident_b")
+        make_identity(nc, ident_b[:])
+
+        warm = const.tile([P, 1], F32, name="warm")
+        nc.vector.memset(warm[:], 0.0)
+        warm_out = const.tile([P, 1], F32, name="warm_out")
+        nc.scalar.activation(out=warm_out[:], in_=warm[:], func=ACT.Sigmoid)
+
+        def transpose_words(src, grouped, copy):
+            words = src[:].bitcast(F32)
+            out_words = grouped[:].bitcast(F32).rearrange("q (s c u) -> q s c u", s=4, u=2)
+            for half in range(2):
+                bank = ps_t.tile([P, 512], F32, name="bank", tag="tp")
+                for s in range(2):
+                    for u in range(2):
+                        first = (2 * half + s) * 256 + u * P
+                        nc.tensor.transpose(
+                            bank[:, (2 * s + u) * P : (2 * s + u + 1) * P], words[:, first : first + P], ident_f[:]
+                        )
+                copy(
+                    out=out_words[:, 2 * half : 2 * half + 2],
+                    in_=bank[:].rearrange("q (s u c) -> q s c u", s=2, u=2),
+                )
+
+        w_grouped = const.tile([P, 4 * P * 4], BF16, name="w_grouped", align_bytes=64)
+        transpose_words(w_sb, w_grouped, nc.vector.tensor_copy)
+        w_codes = const.tile([P, 4 * P], U32, name="w_codes", align_bytes=64)
+        w_scales = const.tile([P, 4 * P], U8, name="w_scales", align_bytes=64)
+        nc.vector.quantize_mx(out=w_codes[:].bitcast(FP8X4), scales=w_scales[:], in_=w_grouped[:])
+
+        ut = ps_t.tile([P, 4 * HID], BF16, name="ut", tag="tp")
+        for n in range(4):
+            nc.tensor.transpose(ut[:, n * HID : (n + 1) * HID], u_sb[:, n * HID : (n + 1) * HID], ident_b[:])
+        u_t = const.tile([P, 4 * HID], BF16, name="u_t")
+        nc.vector.tensor_copy(out=u_t[:], in_=ut[:])
+
+        bt = ps_t.tile([P, P], BF16, name="bt", tag="tp")
+        nc.tensor.transpose(bt[:], b_rows[:], ident_b[:])
+        bias_col = const.tile([P, 4], F32, name="bias_col")
+        nc.vector.tensor_copy(out=bias_col[:], in_=bt[:, 0:4])
+
+        grouped = {}
+        codes = {}
+        scales = {}
+        h_t_sb = {}
+        a_sb = {}
+        acts = {}
+        cell = {}
+        tanh_c = {}
+
+        def stage_tx(j):
+            grouped[j] = work2.tile([P, GW * 4], BF16, name="grouped", align_bytes=64)
+            transpose_words(x_sb[j], grouped[j], nc.scalar.copy)
+
+        def stage_th(j):
+            src = h_sb[j // HC]
+            base = (j % HC) * GW
+            ht = ps_t.tile([P, GW], BF16, name="ht", tag="tp")
+            for s in range(GT):
+                nc.tensor.transpose(ht[:, s * P : (s + 1) * P], src[:, base + s * P : base + (s + 1) * P], ident_b[:])
+            h_t_sb[j] = work4.tile([P, GW], BF16, name="h_t_sb")
+            nc.vector.tensor_copy(out=h_t_sb[j][:], in_=ht[:])
+
+        def stage_q(j):
+            codes[j] = work3.tile([P, GW], U32, name="codes", align_bytes=64)
+            scales[j] = work3.tile([P, GW], U8, name="scales", align_bytes=64)
+            nc.vector.quantize_mx(out=codes[j][:].bitcast(FP8X4), scales=scales[j][:], in_=grouped[j][:])
+
+        def stage_mx(j):
+            a_sb[j] = work2.tile([P, 4 * GW], F32, name="a_sb")
+            for n in range(4):
+                mx = ps_mx.tile([P, GW], F32, name="mx", tag="mx")
+                nc.tensor.matmul_mx(
+                    out=mx[:],
+                    lhsT=w_codes[:, n * P : (n + 1) * P].bitcast(FP8X4),
+                    lhsT_scale=w_scales[:, n * P : (n + 1) * P],
+                    rhs=codes[j][:].bitcast(FP8X4),
+                    rhs_scale=scales[j][:],
+                    start=True,
+                    stop=True,
+                )
+                nc.vector.tensor_scalar_add(
+                    out=a_sb[j][:, n * GW : (n + 1) * GW], in0=mx[:], scalar1=bias_col[:, n : n + 1]
+                )
+
+        def stage_g(j):
+            acts[j] = work4.tile([P, GT * 4 * HID], F32, name="acts")
+            for s in range(GT):
+                g = ps_g.tile([P, 4 * HID], F32, name="g", tag="g")
+                nc.tensor.matmul(
+                    out=g[:], lhsT=h_t_sb[j][:, s * P : (s + 1) * P], rhs=u_t[:], start=True, stop=False
+                )
+                for n in range(4):
+                    nc.tensor.matmul(
+                        out=g[:, n * HID : (n + 1) * HID],
+                        lhsT=a_sb[j][:, n * GW + s * P : n * GW + (s + 1) * P],
+                        rhs=ident_f[:],
+                        is_transpose=True,
+                        start=False,
+                        stop=(n == 3),
+                    )
+                base = s * 4 * HID
+                nc.scalar.activation(out=acts[j][:, base : base + 3 * HID], in_=g[:, 0 : 3 * HID], func=ACT.Sigmoid)
+                nc.scalar.activation(
+                    out=acts[j][:, base + 3 * HID : base + 4 * HID], in_=g[:, 3 * HID : 4 * HID], func=ACT.Tanh
+                )
+
+        def by_tile(ap):
+            return ap.rearrange("p (t h) -> p t h", t=GT)
+
+        def stage_cell(j):
+            av = acts[j][:].rearrange("p (t n h) -> p t n h", t=GT, n=4)
+            c_old = c_sb[j // HC][:, (j % HC) * GW : (j % HC + 1) * GW]
+            fc = work2.tile([P, GW], F32, name="fc")
+            ic = work2.tile([P, GW], F32, name="ic")
+            nc.gpsimd.tensor_tensor(out=by_tile(fc[:]), in0=av[:, :, 1, :], in1=by_tile(c_old), op=ALU.mult)
+            nc.gpsimd.tensor_tensor(out=by_tile(ic[:]), in0=av[:, :, 0, :], in1=av[:, :, 3, :], op=ALU.mult)
+            cell[j] = work3.tile([P, GW], F32, name="cell")
+            nc.vector.tensor_tensor(out=cell[j][:], in0=fc[:], in1=ic[:], op=ALU.add)
+            nc.sync.dma_start(out=ncell_rows[:, j * GW : (j + 1) * GW], in_=cell[j][:])
+
+        def stage_tanh(j):
+            tanh_c[j] = work2.tile([P, GW], F32, name="tanh_c")
+            nc.scalar.activation(out=tanh_c[j][:], in_=cell[j][:], func=ACT.Tanh)
+
+        def stage_h(j):
+            av = acts[j][:].rearrange("p (t n h) -> p t n h", t=GT, n=4)
+            nh = work3.tile([P, GW], F32, name="nh")
+            nc.vector.tensor_tensor(out=by_tile(nh[:]), in0=av[:, :, 2, :], in1=by_tile(tanh_c[j][:]), op=ALU.mult)
+            nc.sync.dma_start(out=nh_rows[:, j * GW : (j + 1) * GW], in_=nh[:])
+
+        stage_tx(0)
+        stage_th(0)
+        stage_q(0)
+        stage_tx(1)
+        stage_th(1)
+        stage_mx(0)
+        stage_q(1)
+        for i in range(NG + 2):
+            if i + 2 < NG:
+                stage_tx(i + 2)
+                stage_th(i + 2)
+            if 0 <= i - 2:
+                stage_tanh(i - 2)
+            if i + 1 < NG:
+                stage_mx(i + 1)
+            if i + 2 < NG:
+                stage_q(i + 2)
+            if 0 <= i - 1 < NG:
+                stage_cell(i - 1)
+            if 0 <= i - 2:
+                stage_h(i - 2)
+            if i < NG:
+                stage_g(i)

@@ -160,9 +160,14 @@ def tile_lstmcell_t_kernel(
                     start=True,
                     stop=True,
                 )
-                nc.vector.tensor_scalar_add(
-                    out=a_sb[j][:, n * GW : (n + 1) * GW], in0=mx[:], scalar1=bias_col[:, n : n + 1]
-                )
+                if n == 1:
+                    nc.scalar.activation(
+                        out=a_sb[j][:, n * GW : (n + 1) * GW], in_=mx[:], func=ACT.Identity, bias=bias_col[:, n : n + 1]
+                    )
+                else:
+                    nc.vector.tensor_scalar_add(
+                        out=a_sb[j][:, n * GW : (n + 1) * GW], in0=mx[:], scalar1=bias_col[:, n : n + 1]
+                    )
 
         def stage_g(j):
             acts[j] = work4.tile([P, GT * 4 * HID], F32, name="acts")
@@ -194,8 +199,8 @@ def tile_lstmcell_t_kernel(
             c_old = c_sb[j // HC][:, (j % HC) * GW : (j % HC + 1) * GW]
             fc = work2.tile([P, GW], F32, name="fc")
             ic = work2.tile([P, GW], F32, name="ic")
-            nc.gpsimd.tensor_tensor(out=by_tile(fc[:]), in0=av[:, :, 1, :], in1=by_tile(c_old), op=ALU.mult)
-            nc.gpsimd.tensor_tensor(out=by_tile(ic[:]), in0=av[:, :, 0, :], in1=av[:, :, 3, :], op=ALU.mult)
+            nc.vector.tensor_tensor(out=by_tile(fc[:]), in0=av[:, :, 1, :], in1=by_tile(c_old), op=ALU.mult)
+            nc.vector.tensor_tensor(out=by_tile(ic[:]), in0=av[:, :, 0, :], in1=av[:, :, 3, :], op=ALU.mult)
             cell[j] = work3.tile([P, GW], F32, name="cell")
             nc.vector.tensor_tensor(out=cell[j][:], in0=fc[:], in1=ic[:], op=ALU.add)
             nc.sync.dma_start(out=ncell_rows[:, j * GW : (j + 1) * GW], in_=cell[j][:])

@@ -44,38 +44,8 @@ def tile_lstmcell_t_kernel(
         work2 = ctx.enter_context(tc.tile_pool(name="work2", bufs=2))
         work3 = ctx.enter_context(tc.tile_pool(name="work3", bufs=3))
         work4 = ctx.enter_context(tc.tile_pool(name="work4", bufs=4))
-        ps_t = ctx.enter_context(tc.psum_pool(name="ps_t", bufs=3))
-        ps_mx = ctx.enter_context(tc.psum_pool(name="ps_mx", bufs=3))
-        ps_g = ctx.enter_context(tc.psum_pool(name="ps_g", bufs=2))
-
-        w_sb = const.tile([P, 4 * IN_F], BF16, name="w_sb")
-        for n in range(4):
-            nc.sync.dma_start(out=w_sb[:, n * IN_F : (n + 1) * IN_F], in_=gate_w[n])
-        u_sb = const.tile([P, 4 * HID], BF16, name="u_sb")
-        for n in range(4):
-            nc.scalar.dma_start(out=u_sb[:, n * HID : (n + 1) * HID], in_=gate_u[n])
-        b_rows = const.tile([P, P], BF16, name="b_rows")
-        nc.vector.memset(b_rows[:], 0.0)
-        for n in range(4):
-            nc.scalar.dma_start(out=b_rows[n : n + 1, :], in_=gate_b[n].rearrange("(o h) -> o h", o=1))
-
-        x_sb = []
-        h_sb = []
-        c_sb = []
-        for j in range(NG):
-            x_t = resident.tile([P, GT * IN_F], BF16, name="x%d" % j)
-            nc.sync.dma_start(out=x_t[:], in_=x_rows[:, j * GT * IN_F : (j + 1) * GT * IN_F])
-            x_sb.append(x_t)
-            if j % HC == 0:
-                m = j // HC
-                h_t = resident.tile([P, HC * GW], BF16, name="h%d" % m)
-                nc.sync.dma_start(out=h_t[:], in_=h_rows[:, m * HC * GW : (m + 1) * HC * GW])
-                h_sb.append(h_t)
-            if j % HC == 1:
-                m = j // HC
-                c_t = resident.tile([P, HC * GW], BF16, name="c%d" % m)
-                nc.sync.dma_start(out=c_t[:], in_=c_rows[:, m * HC * GW : (m + 1) * HC * GW])
-                c_sb.append(c_t)
+        psum = ctx.enter_context(tc.psum_pool(name="psum", bufs=8))
+        ctx.enter_context(tc.manual_schedule())
 
         ident_f = const.tile([P, P], F32, name="ident_f")
         make_identity(nc, ident_f[:])
@@ -87,11 +57,51 @@ def tile_lstmcell_t_kernel(
         warm_out = const.tile([P, 1], F32, name="warm_out")
         nc.scalar.activation(out=warm_out[:], in_=warm[:], func=ACT.Sigmoid)
 
+        x_sb = []
+        h_sb = []
+        c_sb = []
+
+        def load_x(j):
+            x_t = resident.tile([P, GT * IN_F], BF16, name="x%d" % j)
+            nc.sync.dma_start(out=x_t[:], in_=x_rows[:, j * GT * IN_F : (j + 1) * GT * IN_F])
+            x_sb.append(x_t)
+
+        def load_h(m):
+            h_t = resident.tile([P, HC * GW], BF16, name="h%d" % m)
+            nc.sync.dma_start(out=h_t[:], in_=h_rows[:, m * HC * GW : (m + 1) * HC * GW])
+            h_sb.append(h_t)
+
+        def load_c(m):
+            c_t = resident.tile([P, HC * GW], BF16, name="c%d" % m)
+            nc.sync.dma_start(out=c_t[:], in_=c_rows[:, m * HC * GW : (m + 1) * HC * GW])
+            c_sb.append(c_t)
+
+        w_sb = const.tile([P, 4 * IN_F], BF16, name="w_sb")
+        for n in range(4):
+            nc.sync.dma_start(out=w_sb[:, n * IN_F : (n + 1) * IN_F], in_=gate_w[n])
+        load_x(0)
+        load_h(0)
+        u_sb = const.tile([P, 4 * HID], BF16, name="u_sb")
+        for n in range(4):
+            nc.scalar.dma_start(out=u_sb[:, n * HID : (n + 1) * HID], in_=gate_u[n])
+        b_rows = const.tile([P, P], BF16, name="b_rows")
+        nc.vector.memset(b_rows[:], 0.0)
+        for n in range(4):
+            nc.scalar.dma_start(out=b_rows[n : n + 1, :], in_=gate_b[n].rearrange("(o h) -> o h", o=1))
+        load_x(1)
+        load_c(0)
+        for j in range(2, NG):
+            load_x(j)
+            if j % HC == 2 and j // HC + 1 < NG // HC:
+                load_h(j // HC + 1)
+            if j % HC == 3 and j // HC + 1 < NG // HC:
+                load_c(j // HC + 1)
+
         def transpose_words(src, grouped, copy):
             words = src[:].bitcast(F32)
             out_words = grouped[:].bitcast(F32).rearrange("q (s c u) -> q s c u", s=4, u=2)
             for half in range(2):
-                bank = ps_t.tile([P, 512], F32, name="bank", tag="tp")
+                bank = psum.tile([P, 512], F32, name="bank", tag="bank")
                 for s in range(2):
                     for u in range(2):
                         first = (2 * half + s) * 256 + u * P
@@ -109,17 +119,6 @@ def tile_lstmcell_t_kernel(
         w_scales = const.tile([P, 4 * P], U8, name="w_scales", align_bytes=64)
         nc.vector.quantize_mx(out=w_codes[:].bitcast(FP8X4), scales=w_scales[:], in_=w_grouped[:])
 
-        ut = ps_t.tile([P, 4 * HID], BF16, name="ut", tag="tp")
-        for n in range(4):
-            nc.tensor.transpose(ut[:, n * HID : (n + 1) * HID], u_sb[:, n * HID : (n + 1) * HID], ident_b[:])
-        u_t = const.tile([P, 4 * HID], BF16, name="u_t")
-        nc.vector.tensor_copy(out=u_t[:], in_=ut[:])
-
-        bt = ps_t.tile([P, P], BF16, name="bt", tag="tp")
-        nc.tensor.transpose(bt[:], b_rows[:], ident_b[:])
-        bias_col = const.tile([P, 4], F32, name="bias_col")
-        nc.vector.tensor_copy(out=bias_col[:], in_=bt[:, 0:4])
-
         grouped = {}
         codes = {}
         scales = {}
@@ -136,7 +135,7 @@ def tile_lstmcell_t_kernel(
         def stage_th(j):
             src = h_sb[j // HC]
             base = (j % HC) * GW
-            ht = ps_t.tile([P, GW], BF16, name="ht", tag="tp")
+            ht = psum.tile([P, GW], BF16, name="ht", tag="bank")
             for s in range(GT):
                 nc.tensor.transpose(ht[:, s * P : (s + 1) * P], src[:, base + s * P : base + (s + 1) * P], ident_b[:])
             h_t_sb[j] = work4.tile([P, GW], BF16, name="h_t_sb")
@@ -150,7 +149,7 @@ def tile_lstmcell_t_kernel(
         def stage_mx(j):
             a_sb[j] = work2.tile([P, 4 * GW], F32, name="a_sb")
             for n in range(4):
-                mx = ps_mx.tile([P, GW], F32, name="mx", tag="mx")
+                mx = psum.tile([P, GW], F32, name="mx", tag="bank")
                 nc.tensor.matmul_mx(
                     out=mx[:],
                     lhsT=w_codes[:, n * P : (n + 1) * P].bitcast(FP8X4),
@@ -160,31 +159,26 @@ def tile_lstmcell_t_kernel(
                     start=True,
                     stop=True,
                 )
-                if n == 1:
-                    nc.scalar.activation(
-                        out=a_sb[j][:, n * GW : (n + 1) * GW], in_=mx[:], func=ACT.Identity, bias=bias_col[:, n : n + 1]
-                    )
-                else:
-                    nc.vector.tensor_scalar_add(
-                        out=a_sb[j][:, n * GW : (n + 1) * GW], in0=mx[:], scalar1=bias_col[:, n : n + 1]
-                    )
+                nc.vector.tensor_scalar_add(
+                    out=a_sb[j][:, n * GW : (n + 1) * GW], in0=mx[:], scalar1=bias_col[:, n : n + 1]
+                )
 
         def stage_g(j):
             acts[j] = work4.tile([P, GT * 4 * HID], F32, name="acts")
             for s in range(GT):
-                g = ps_g.tile([P, 4 * HID], F32, name="g", tag="g")
-                nc.tensor.matmul(
-                    out=g[:], lhsT=h_t_sb[j][:, s * P : (s + 1) * P], rhs=u_t[:], start=True, stop=False
-                )
+                g = psum.tile([P, 4 * HID], F32, name="g", tag="bank")
                 for n in range(4):
                     nc.tensor.matmul(
                         out=g[:, n * HID : (n + 1) * HID],
                         lhsT=a_sb[j][:, n * GW + s * P : n * GW + (s + 1) * P],
                         rhs=ident_f[:],
                         is_transpose=True,
-                        start=False,
-                        stop=(n == 3),
+                        start=(n == 0),
+                        stop=False,
                     )
+                nc.tensor.matmul(
+                    out=g[:], lhsT=h_t_sb[j][:, s * P : (s + 1) * P], rhs=u_t[:], start=False, stop=True
+                )
                 base = s * 4 * HID
                 nc.scalar.activation(out=acts[j][:, base : base + 3 * HID], in_=g[:, 0 : 3 * HID], func=ACT.Sigmoid)
                 nc.scalar.activation(
@@ -199,8 +193,9 @@ def tile_lstmcell_t_kernel(
             c_old = c_sb[j // HC][:, (j % HC) * GW : (j % HC + 1) * GW]
             fc = work2.tile([P, GW], F32, name="fc")
             ic = work2.tile([P, GW], F32, name="ic")
-            nc.vector.tensor_tensor(out=by_tile(fc[:]), in0=av[:, :, 1, :], in1=by_tile(c_old), op=ALU.mult)
-            nc.vector.tensor_tensor(out=by_tile(ic[:]), in0=av[:, :, 0, :], in1=av[:, :, 3, :], op=ALU.mult)
+            eng = nc.vector if j == NG - 1 else nc.gpsimd
+            eng.tensor_tensor(out=by_tile(fc[:]), in0=av[:, :, 1, :], in1=by_tile(c_old), op=ALU.mult)
+            eng.tensor_tensor(out=by_tile(ic[:]), in0=av[:, :, 0, :], in1=av[:, :, 3, :], op=ALU.mult)
             cell[j] = work3.tile([P, GW], F32, name="cell")
             nc.vector.tensor_tensor(out=cell[j][:], in0=fc[:], in1=ic[:], op=ALU.add)
             nc.sync.dma_start(out=ncell_rows[:, j * GW : (j + 1) * GW], in_=cell[j][:])
@@ -217,6 +212,16 @@ def tile_lstmcell_t_kernel(
 
         stage_tx(0)
         stage_th(0)
+        ut = psum.tile([P, 4 * HID], BF16, name="ut", tag="bank")
+        for n in range(4):
+            nc.tensor.transpose(ut[:, n * HID : (n + 1) * HID], u_sb[:, n * HID : (n + 1) * HID], ident_b[:])
+        u_t = const.tile([P, 4 * HID], BF16, name="u_t")
+        nc.vector.tensor_copy(out=u_t[:], in_=ut[:])
+
+        bt = psum.tile([P, P], BF16, name="bt", tag="bank")
+        nc.tensor.transpose(bt[:], b_rows[:], ident_b[:])
+        bias_col = const.tile([P, 4], F32, name="bias_col")
+        nc.vector.tensor_copy(out=bias_col[:], in_=bt[:, 0:4])
         stage_q(0)
         stage_tx(1)
         stage_th(1)

@@ -18,8 +18,8 @@ HID = 128
 NT = BATCH // P
 GT = 4
 NG = NT // GT
-HC = 4
 GW = GT * P
+HC_SIZES = [2, 2, 4, 4, 4]
 
 FLOPS = 2 * BATCH * (IN_F + HID) * 4 * HID
 
@@ -36,7 +36,7 @@ def tile_lstmcell_t_kernel(
     h_rows = old_h.rearrange("(p t) k -> p (t k)", t=NT)
     c_rows = old_c.rearrange("(p t) k -> p (t k)", t=NT)
     nh_rows = out_0.rearrange("(p t) k -> p (t k)", t=NT)
-    ncell_rows = out_1.rearrange("(p t) k -> p (t k)", t=NT)
+    cell_rows = out_1.rearrange("(p t) k -> p (t k)", t=NT)
 
     with ExitStack() as ctx:
         const = ctx.enter_context(tc.tile_pool(name="const", bufs=1))
@@ -57,24 +57,26 @@ def tile_lstmcell_t_kernel(
         warm_out = const.tile([P, 1], F32, name="warm_out")
         nc.scalar.activation(out=warm_out[:], in_=warm[:], func=ACT.Sigmoid)
 
-        x_sb = []
-        h_sb = []
-        c_sb = []
+        x_sb = {}
+        h_of = {}
+        c_of = {}
 
         def load_x(j):
-            x_t = resident.tile([P, GT * IN_F], BF16, name="x%d" % j)
-            nc.sync.dma_start(out=x_t[:], in_=x_rows[:, j * GT * IN_F : (j + 1) * GT * IN_F])
-            x_sb.append(x_t)
+            x_sb[j] = resident.tile([P, GT * IN_F], BF16, name="x%d" % j)
+            nc.sync.dma_start(out=x_sb[j][:], in_=x_rows[:, j * GT * IN_F : (j + 1) * GT * IN_F])
+
+        def load_hc(m, rows, table, letter):
+            first = sum(HC_SIZES[:m])
+            t = resident.tile([P, HC_SIZES[m] * GW], BF16, name="%s%d" % (letter, m))
+            nc.sync.dma_start(out=t[:], in_=rows[:, first * GW : (first + HC_SIZES[m]) * GW])
+            for r in range(HC_SIZES[m]):
+                table[first + r] = t[:, r * GW : (r + 1) * GW]
 
         def load_h(m):
-            h_t = resident.tile([P, HC * GW], BF16, name="h%d" % m)
-            nc.sync.dma_start(out=h_t[:], in_=h_rows[:, m * HC * GW : (m + 1) * HC * GW])
-            h_sb.append(h_t)
+            load_hc(m, h_rows, h_of, "h")
 
         def load_c(m):
-            c_t = resident.tile([P, HC * GW], BF16, name="c%d" % m)
-            nc.sync.dma_start(out=c_t[:], in_=c_rows[:, m * HC * GW : (m + 1) * HC * GW])
-            c_sb.append(c_t)
+            load_hc(m, c_rows, c_of, "c")
 
         w_sb = const.tile([P, 4 * IN_F], BF16, name="w_sb")
         for n in range(4):
@@ -89,15 +91,31 @@ def tile_lstmcell_t_kernel(
         for n in range(4):
             nc.scalar.dma_start(out=b_rows[n : n + 1, :], in_=gate_b[n].rearrange("(o h) -> o h", o=1))
         load_x(1)
+        load_x(2)
         load_c(0)
-        for j in range(2, NG):
-            load_x(j)
-            if j % HC == 2 and j // HC + 1 < NG // HC:
-                load_h(j // HC + 1)
-            if j % HC == 3 and j // HC + 1 < NG // HC:
-                load_c(j // HC + 1)
+        load_h(1)
+        load_x(3)
+        load_c(1)
+        load_x(4)
+        load_h(2)
+        load_x(5)
+        load_c(2)
+        load_x(6)
+        load_x(7)
+        load_x(8)
+        load_h(3)
+        load_c(3)
+        load_x(9)
+        load_x(10)
+        load_x(11)
+        load_x(12)
+        load_h(4)
+        load_c(4)
+        load_x(13)
+        load_x(14)
+        load_x(15)
 
-        def transpose_words(src, grouped, copy):
+        def transpose_words(src, grouped, copies):
             words = src[:].bitcast(F32)
             out_words = grouped[:].bitcast(F32).rearrange("q (s c u) -> q s c u", s=4, u=2)
             for half in range(2):
@@ -108,16 +126,10 @@ def tile_lstmcell_t_kernel(
                         nc.tensor.transpose(
                             bank[:, (2 * s + u) * P : (2 * s + u + 1) * P], words[:, first : first + P], ident_f[:]
                         )
-                copy(
+                copies[half](
                     out=out_words[:, 2 * half : 2 * half + 2],
                     in_=bank[:].rearrange("q (s u c) -> q s c u", s=2, u=2),
                 )
-
-        w_grouped = const.tile([P, 4 * P * 4], BF16, name="w_grouped", align_bytes=64)
-        transpose_words(w_sb, w_grouped, nc.vector.tensor_copy)
-        w_codes = const.tile([P, 4 * P], U32, name="w_codes", align_bytes=64)
-        w_scales = const.tile([P, 4 * P], U8, name="w_scales", align_bytes=64)
-        nc.vector.quantize_mx(out=w_codes[:].bitcast(FP8X4), scales=w_scales[:], in_=w_grouped[:])
 
         grouped = {}
         codes = {}
@@ -125,19 +137,19 @@ def tile_lstmcell_t_kernel(
         h_t_sb = {}
         a_sb = {}
         acts = {}
+        fc = {}
+        ic = {}
         cell = {}
         tanh_c = {}
 
-        def stage_tx(j):
+        def stage_tx(j, copies):
             grouped[j] = work2.tile([P, GW * 4], BF16, name="grouped", align_bytes=64)
-            transpose_words(x_sb[j], grouped[j], nc.scalar.copy)
+            transpose_words(x_sb[j], grouped[j], copies)
 
         def stage_th(j):
-            src = h_sb[j // HC]
-            base = (j % HC) * GW
             ht = psum.tile([P, GW], BF16, name="ht", tag="bank")
             for s in range(GT):
-                nc.tensor.transpose(ht[:, s * P : (s + 1) * P], src[:, base + s * P : base + (s + 1) * P], ident_b[:])
+                nc.tensor.transpose(ht[:, s * P : (s + 1) * P], h_of[j][:, s * P : (s + 1) * P], ident_b[:])
             h_t_sb[j] = work4.tile([P, GW], BF16, name="h_t_sb")
             nc.vector.tensor_copy(out=h_t_sb[j][:], in_=ht[:])
 
@@ -146,8 +158,8 @@ def tile_lstmcell_t_kernel(
             scales[j] = work3.tile([P, GW], U8, name="scales", align_bytes=64)
             nc.vector.quantize_mx(out=codes[j][:].bitcast(FP8X4), scales=scales[j][:], in_=grouped[j][:])
 
-        def stage_mx(j):
-            a_sb[j] = work2.tile([P, 4 * GW], F32, name="a_sb")
+        def stage_mx(j, on_scalar):
+            a_sb[j] = work3.tile([P, 4 * GW], F32, name="a_sb")
             for n in range(4):
                 mx = psum.tile([P, GW], F32, name="mx", tag="bank")
                 nc.tensor.matmul_mx(
@@ -159,13 +171,19 @@ def tile_lstmcell_t_kernel(
                     start=True,
                     stop=True,
                 )
-                nc.vector.tensor_scalar_add(
-                    out=a_sb[j][:, n * GW : (n + 1) * GW], in0=mx[:], scalar1=bias_col[:, n : n + 1]
-                )
+                if n in on_scalar:
+                    nc.scalar.activation(
+                        out=a_sb[j][:, n * GW : (n + 1) * GW], in_=mx[:], func=ACT.Identity, bias=bias_col[:, n : n + 1]
+                    )
+                else:
+                    nc.vector.tensor_scalar_add(
+                        out=a_sb[j][:, n * GW : (n + 1) * GW], in0=mx[:], scalar1=bias_col[:, n : n + 1]
+                    )
 
-        def stage_g(j):
-            acts[j] = work4.tile([P, GT * 4 * HID], F32, name="acts")
-            for s in range(GT):
+        def stage_g(j, s0, s1):
+            if s0 == 0:
+                acts[j] = work3.tile([P, GT * 4 * HID], F32, name="acts")
+            for s in range(s0, s1):
                 g = psum.tile([P, 4 * HID], F32, name="g", tag="bank")
                 for n in range(4):
                     nc.tensor.matmul(
@@ -185,61 +203,116 @@ def tile_lstmcell_t_kernel(
                     out=acts[j][:, base + 3 * HID : base + 4 * HID], in_=g[:, 3 * HID : 4 * HID], func=ACT.Tanh
                 )
 
-        def by_tile(ap):
-            return ap.rearrange("p (t h) -> p t h", t=GT)
+        def by_tile(ap, tiles):
+            return ap.rearrange("p (t h) -> p t h", t=tiles)
 
-        def stage_cell(j):
-            av = acts[j][:].rearrange("p (t n h) -> p t n h", t=GT, n=4)
-            c_old = c_sb[j // HC][:, (j % HC) * GW : (j % HC + 1) * GW]
-            fc = work2.tile([P, GW], F32, name="fc")
-            ic = work2.tile([P, GW], F32, name="ic")
-            eng = nc.vector if j == NG - 1 else nc.gpsimd
-            eng.tensor_tensor(out=by_tile(fc[:]), in0=av[:, :, 1, :], in1=by_tile(c_old), op=ALU.mult)
-            eng.tensor_tensor(out=by_tile(ic[:]), in0=av[:, :, 0, :], in1=av[:, :, 3, :], op=ALU.mult)
-            cell[j] = work3.tile([P, GW], F32, name="cell")
-            nc.vector.tensor_tensor(out=cell[j][:], in0=fc[:], in1=ic[:], op=ALU.add)
-            nc.sync.dma_start(out=ncell_rows[:, j * GW : (j + 1) * GW], in_=cell[j][:])
+        def gate(j, n, s0, s1):
+            return acts[j][:].rearrange("p (t n h) -> p t n h", t=GT, n=4)[:, s0:s1, n, :]
 
-        def stage_tanh(j):
-            tanh_c[j] = work2.tile([P, GW], F32, name="tanh_c")
-            nc.scalar.activation(out=tanh_c[j][:], in_=cell[j][:], func=ACT.Tanh)
+        def stage_prod(j, eng, s0, s1):
+            tiles = s1 - s0
+            key = (j, s0)
+            fc[key] = work2.tile([P, tiles * HID], F32, name="fc")
+            ic[key] = work2.tile([P, tiles * HID], F32, name="ic")
+            eng.tensor_tensor(
+                out=by_tile(fc[key][:], tiles),
+                in0=gate(j, 1, s0, s1),
+                in1=by_tile(c_of[j][:, s0 * HID : s1 * HID], tiles),
+                op=ALU.mult,
+            )
+            eng.tensor_tensor(out=by_tile(ic[key][:], tiles), in0=gate(j, 0, s0, s1), in1=gate(j, 3, s0, s1), op=ALU.mult)
 
-        def stage_h(j):
-            av = acts[j][:].rearrange("p (t n h) -> p t n h", t=GT, n=4)
-            nh = work3.tile([P, GW], F32, name="nh")
-            nc.vector.tensor_tensor(out=by_tile(nh[:]), in0=av[:, :, 2, :], in1=by_tile(tanh_c[j][:]), op=ALU.mult)
-            nc.sync.dma_start(out=nh_rows[:, j * GW : (j + 1) * GW], in_=nh[:])
+        def stage_add(j, s0, s1):
+            key = (j, s0)
+            cell[key] = work4.tile([P, (s1 - s0) * HID], F32, name="cell")
+            nc.vector.tensor_tensor(out=cell[key][:], in0=fc[key][:], in1=ic[key][:], op=ALU.add)
+            nc.sync.dma_start(out=cell_rows[:, j * GW + s0 * HID : j * GW + s1 * HID], in_=cell[key][:])
 
-        stage_tx(0)
+        def stage_tanh(j, s0, s1):
+            key = (j, s0)
+            tanh_c[key] = work2.tile([P, (s1 - s0) * HID], F32, name="tanh_c")
+            nc.scalar.activation(out=tanh_c[key][:], in_=cell[key][:], func=ACT.Tanh)
+
+        def stage_h(j, s0, s1):
+            tiles = s1 - s0
+            nh = work4.tile([P, tiles * HID], F32, name="nh")
+            nc.vector.tensor_tensor(
+                out=by_tile(nh[:], tiles), in0=gate(j, 2, s0, s1), in1=by_tile(tanh_c[(j, s0)][:], tiles), op=ALU.mult
+            )
+            nc.sync.dma_start(out=nh_rows[:, j * GW + s0 * HID : j * GW + s1 * HID], in_=nh[:])
+
+        on_s = [nc.scalar.copy, nc.scalar.copy]
+
+        w_grouped = const.tile([P, 4 * P * 4], BF16, name="w_grouped", align_bytes=64)
+        transpose_words(w_sb, w_grouped, [nc.vector.tensor_copy, nc.vector.tensor_copy])
+        w_codes = const.tile([P, 4 * P], U32, name="w_codes", align_bytes=64)
+        w_scales = const.tile([P, 4 * P], U8, name="w_scales", align_bytes=64)
+        nc.vector.quantize_mx(out=w_codes[:].bitcast(FP8X4), scales=w_scales[:], in_=w_grouped[:])
+
+        stage_tx(0, [nc.scalar.copy, nc.vector.tensor_copy])
         stage_th(0)
+
         ut = psum.tile([P, 4 * HID], BF16, name="ut", tag="bank")
         for n in range(4):
             nc.tensor.transpose(ut[:, n * HID : (n + 1) * HID], u_sb[:, n * HID : (n + 1) * HID], ident_b[:])
         u_t = const.tile([P, 4 * HID], BF16, name="u_t")
         nc.vector.tensor_copy(out=u_t[:], in_=ut[:])
-
         bt = psum.tile([P, P], BF16, name="bt", tag="bank")
         nc.tensor.transpose(bt[:], b_rows[:], ident_b[:])
         bias_col = const.tile([P, 4], F32, name="bias_col")
         nc.vector.tensor_copy(out=bias_col[:], in_=bt[:, 0:4])
+
         stage_q(0)
-        stage_tx(1)
+        stage_tx(1, on_s)
         stage_th(1)
-        stage_mx(0)
+        stage_mx(0, [1, 3])
         stage_q(1)
-        for i in range(NG + 2):
+        stage_tx(2, on_s)
+        stage_th(2)
+        stage_mx(1, [])
+        stage_q(2)
+        for i in range(NG - 2):
+            if i + 3 < NG:
+                stage_tx(i + 3, on_s)
+                stage_th(i + 3)
+            if i >= 1:
+                stage_prod(i - 1, nc.gpsimd, 0, GT)
+            if i + 3 < NG:
+                stage_q(i + 3)
+            if i >= 1:
+                stage_add(i - 1, 0, GT)
+            if i >= 2:
+                stage_h(i - 2, 0, GT)
+            stage_g(i, 0, GT)
+            if i >= 1:
+                stage_tanh(i - 1, 0, GT)
             if i + 2 < NG:
-                stage_tx(i + 2)
-                stage_th(i + 2)
-            if 0 <= i - 2:
-                stage_tanh(i - 2)
-            if i + 1 < NG:
-                stage_mx(i + 1)
-            if i + 2 < NG:
-                stage_q(i + 2)
-            if 0 <= i - 1 < NG:
-                stage_cell(i - 1)
-            if 0 <= i - 2:
-                stage_h(i - 2)
-            if i < NG:
-                stage_g(i)
+                stage_mx(i + 2, [])
+
+        ga = NG - 3
+        gb = NG - 2
+        gc = NG - 1
+        stage_prod(ga, nc.gpsimd, 0, GT)
+        stage_g(gb, 0, 4)
+        stage_h(ga - 1, 0, GT)
+        stage_prod(gb, nc.vector, 0, 2)
+        stage_add(gb, 0, 2)
+        stage_add(ga, 0, GT)
+        stage_g(gc, 0, 2)
+        stage_tanh(ga, 0, GT)
+        stage_prod(gb, nc.vector, 2, 4)
+        stage_add(gb, 2, 4)
+        stage_tanh(gb, 0, 2)
+        stage_h(ga, 0, GT)
+        stage_g(gc, 2, 4)
+        stage_tanh(gb, 2, 4)
+        stage_h(gb, 0, 2)
+        stage_prod(gc, nc.vector, 0, 2)
+        stage_add(gc, 0, 2)
+        stage_h(gb, 2, 4)
+        stage_tanh(gc, 0, 2)
+        stage_prod(gc, nc.vector, 2, 4)
+        stage_add(gc, 2, 4)
+        stage_h(gc, 0, 2)
+        stage_tanh(gc, 2, 4)
+        stage_h(gc, 2, 4)

@@ -175,6 +175,15 @@ def tile_lstmcell_t_kernel(
                     nc.scalar.activation(
                         out=a_sb[j][:, n * GW : (n + 1) * GW], in_=mx[:], func=ACT.Identity, bias=bias_col[:, n : n + 1]
                     )
+                elif n == 3:
+                    nc.vector.tensor_scalar(
+                        out=a_sb[j][:, n * GW : (n + 1) * GW],
+                        in0=mx[:],
+                        scalar1=bias_col[:, n : n + 1],
+                        scalar2=2.0,
+                        op0=ALU.add,
+                        op1=ALU.mult,
+                    )
                 else:
                     nc.vector.tensor_scalar_add(
                         out=a_sb[j][:, n * GW : (n + 1) * GW], in0=mx[:], scalar1=bias_col[:, n : n + 1]
@@ -198,10 +207,7 @@ def tile_lstmcell_t_kernel(
                     out=g[:], lhsT=h_t_sb[j][:, s * P : (s + 1) * P], rhs=u_t[:], start=False, stop=True
                 )
                 base = s * 4 * HID
-                nc.scalar.activation(out=acts[j][:, base : base + 3 * HID], in_=g[:, 0 : 3 * HID], func=ACT.Sigmoid)
-                nc.scalar.activation(
-                    out=acts[j][:, base + 3 * HID : base + 4 * HID], in_=g[:, 3 * HID : 4 * HID], func=ACT.Tanh
-                )
+                nc.scalar.activation(out=acts[j][:, base : base + 4 * HID], in_=g[:], func=ACT.Sigmoid)
 
         def by_tile(ap, tiles):
             return ap.rearrange("p (t h) -> p t h", t=tiles)
@@ -209,23 +215,36 @@ def tile_lstmcell_t_kernel(
         def gate(j, n, s0, s1):
             return acts[j][:].rearrange("p (t n h) -> p t n h", t=GT, n=4)[:, s0:s1, n, :]
 
-        def stage_prod(j, eng, s0, s1):
+        def stage_fc(j, eng, s0, s1):
             tiles = s1 - s0
             key = (j, s0)
             fc[key] = work2.tile([P, tiles * HID], F32, name="fc")
-            ic[key] = work2.tile([P, tiles * HID], F32, name="ic")
             eng.tensor_tensor(
                 out=by_tile(fc[key][:], tiles),
                 in0=gate(j, 1, s0, s1),
                 in1=by_tile(c_of[j][:, s0 * HID : s1 * HID], tiles),
                 op=ALU.mult,
             )
-            eng.tensor_tensor(out=by_tile(ic[key][:], tiles), in0=gate(j, 0, s0, s1), in1=gate(j, 3, s0, s1), op=ALU.mult)
+
+        def stage_ic(j, s0, s1):
+            tiles = s1 - s0
+            key = (j, s0)
+            ic[key] = work2.tile([P, tiles * HID], F32, name="ic")
+            nc.vector.scalar_tensor_tensor(
+                out=by_tile(ic[key][:], tiles),
+                in0=gate(j, 3, s0, s1),
+                scalar=-0.5,
+                in1=gate(j, 0, s0, s1),
+                op0=ALU.add,
+                op1=ALU.mult,
+            )
 
         def stage_add(j, s0, s1):
             key = (j, s0)
             cell[key] = work4.tile([P, (s1 - s0) * HID], F32, name="cell")
-            nc.vector.tensor_tensor(out=cell[key][:], in0=fc[key][:], in1=ic[key][:], op=ALU.add)
+            nc.vector.scalar_tensor_tensor(
+                out=cell[key][:], in0=ic[key][:], scalar=2.0, in1=fc[key][:], op0=ALU.mult, op1=ALU.add
+            )
             nc.sync.dma_start(out=cell_rows[:, j * GW + s0 * HID : j * GW + s1 * HID], in_=cell[key][:])
 
         def stage_tanh(j, s0, s1):
@@ -233,10 +252,10 @@ def tile_lstmcell_t_kernel(
             tanh_c[key] = work2.tile([P, (s1 - s0) * HID], F32, name="tanh_c")
             nc.scalar.activation(out=tanh_c[key][:], in_=cell[key][:], func=ACT.Tanh)
 
-        def stage_h(j, s0, s1):
+        def stage_h(j, eng, s0, s1):
             tiles = s1 - s0
             nh = work4.tile([P, tiles * HID], F32, name="nh")
-            nc.vector.tensor_tensor(
+            eng.tensor_tensor(
                 out=by_tile(nh[:], tiles), in0=gate(j, 2, s0, s1), in1=by_tile(tanh_c[(j, s0)][:], tiles), op=ALU.mult
             )
             nc.sync.dma_start(out=nh_rows[:, j * GW + s0 * HID : j * GW + s1 * HID], in_=nh[:])
@@ -256,7 +275,8 @@ def tile_lstmcell_t_kernel(
         for n in range(4):
             nc.tensor.transpose(ut[:, n * HID : (n + 1) * HID], u_sb[:, n * HID : (n + 1) * HID], ident_b[:])
         u_t = const.tile([P, 4 * HID], BF16, name="u_t")
-        nc.vector.tensor_copy(out=u_t[:], in_=ut[:])
+        nc.vector.tensor_copy(out=u_t[:, 0 : 3 * HID], in_=ut[:, 0 : 3 * HID])
+        nc.vector.tensor_scalar_mul(out=u_t[:, 3 * HID : 4 * HID], in0=ut[:, 3 * HID : 4 * HID], scalar1=2.0)
         bt = psum.tile([P, P], BF16, name="bt", tag="bank")
         nc.tensor.transpose(bt[:], b_rows[:], ident_b[:])
         bias_col = const.tile([P, 4], F32, name="bias_col")
@@ -265,7 +285,7 @@ def tile_lstmcell_t_kernel(
         stage_q(0)
         stage_tx(1, on_s)
         stage_th(1)
-        stage_mx(0, [1, 3])
+        stage_mx(0, [0, 2])
         stage_q(1)
         stage_tx(2, on_s)
         stage_th(2)
@@ -276,43 +296,46 @@ def tile_lstmcell_t_kernel(
                 stage_tx(i + 3, on_s)
                 stage_th(i + 3)
             if i >= 1:
-                stage_prod(i - 1, nc.gpsimd, 0, GT)
+                stage_fc(i - 1, nc.gpsimd, 0, GT)
             if i + 3 < NG:
                 stage_q(i + 3)
             if i >= 1:
+                stage_ic(i - 1, 0, GT)
                 stage_add(i - 1, 0, GT)
             if i >= 2:
-                stage_h(i - 2, 0, GT)
+                stage_h(i - 2, nc.gpsimd, 0, GT)
             stage_g(i, 0, GT)
             if i >= 1:
                 stage_tanh(i - 1, 0, GT)
             if i + 2 < NG:
                 stage_mx(i + 2, [])
 
+        def cell_on_vector(j, s0, s1):
+            stage_ic(j, s0, s1)
+            stage_fc(j, nc.vector, s0, s1)
+            stage_add(j, s0, s1)
+
         ga = NG - 3
         gb = NG - 2
         gc = NG - 1
-        stage_prod(ga, nc.gpsimd, 0, GT)
+        stage_fc(ga, nc.gpsimd, 0, GT)
         stage_g(gb, 0, 4)
-        stage_h(ga - 1, 0, GT)
-        stage_prod(gb, nc.vector, 0, 2)
-        stage_add(gb, 0, 2)
+        stage_h(ga - 1, nc.vector, 0, GT)
+        stage_ic(ga, 0, GT)
+        cell_on_vector(gb, 0, 2)
         stage_add(ga, 0, GT)
         stage_g(gc, 0, 2)
         stage_tanh(ga, 0, GT)
-        stage_prod(gb, nc.vector, 2, 4)
-        stage_add(gb, 2, 4)
+        cell_on_vector(gb, 2, 4)
         stage_tanh(gb, 0, 2)
-        stage_h(ga, 0, GT)
+        stage_h(ga, nc.vector, 0, GT)
         stage_g(gc, 2, 4)
         stage_tanh(gb, 2, 4)
-        stage_h(gb, 0, 2)
-        stage_prod(gc, nc.vector, 0, 2)
-        stage_add(gc, 0, 2)
-        stage_h(gb, 2, 4)
+        stage_h(gb, nc.vector, 0, 2)
+        cell_on_vector(gc, 0, 2)
+        stage_h(gb, nc.vector, 2, 4)
         stage_tanh(gc, 0, 2)
-        stage_prod(gc, nc.vector, 2, 4)
-        stage_add(gc, 2, 4)
-        stage_h(gc, 0, 2)
+        cell_on_vector(gc, 2, 4)
+        stage_h(gc, nc.vector, 0, 2)
         stage_tanh(gc, 2, 4)
-        stage_h(gc, 2, 4)
+        stage_h(gc, nc.vector, 2, 4)

@@ -28,9 +28,10 @@ def tile_lstmcell_t_kernel(
     tc, incoming, old_h, old_c, w_i, b_i, u_i, w_o, b_o, u_o, w_f, b_f, u_f, w_c, b_c, u_c, out_0, out_1
 ):
     nc = tc.nc
-    gate_w = [w_i, w_f, w_o, w_c]
-    gate_u = [u_i, u_f, u_o, u_c]
-    gate_b = [b_i, b_f, b_o, b_c]
+    gate_w = [w_f, w_i, w_c, w_o]
+    gate_u = [u_f, u_i, u_c, u_o]
+    gate_b = [b_f, b_i, b_c, b_o]
+    gate_func = [ACT.Sigmoid, ACT.Sigmoid, ACT.Tanh, ACT.Sigmoid]
 
     x_rows = incoming.rearrange("(p t) k -> p (t k)", t=NT)
     h_rows = old_h.rearrange("(p t) k -> p (t k)", t=NT)
@@ -137,6 +138,7 @@ def tile_lstmcell_t_kernel(
         h_t_sb = {}
         a_sb = {}
         acts = {}
+        sums = {}
         fc = {}
         ic = {}
         cell = {}
@@ -175,90 +177,62 @@ def tile_lstmcell_t_kernel(
                     nc.scalar.activation(
                         out=a_sb[j][:, n * GW : (n + 1) * GW], in_=mx[:], func=ACT.Identity, bias=bias_col[:, n : n + 1]
                     )
-                elif n == 3:
-                    nc.vector.tensor_scalar(
-                        out=a_sb[j][:, n * GW : (n + 1) * GW],
-                        in0=mx[:],
-                        scalar1=bias_col[:, n : n + 1],
-                        scalar2=2.0,
-                        op0=ALU.add,
-                        op1=ALU.mult,
-                    )
                 else:
                     nc.vector.tensor_scalar_add(
                         out=a_sb[j][:, n * GW : (n + 1) * GW], in0=mx[:], scalar1=bias_col[:, n : n + 1]
                     )
 
-        def stage_g(j, s0, s1):
-            if s0 == 0:
-                acts[j] = work3.tile([P, GT * 4 * HID], F32, name="acts")
-            for s in range(s0, s1):
-                g = psum.tile([P, 4 * HID], F32, name="g", tag="bank")
-                for n in range(4):
-                    nc.tensor.matmul(
-                        out=g[:, n * HID : (n + 1) * HID],
-                        lhsT=a_sb[j][:, n * GW + s * P : n * GW + (s + 1) * P],
-                        rhs=ident_f[:],
-                        is_transpose=True,
-                        start=(n == 0),
-                        stop=False,
-                    )
+        def stage_gacc(j, n):
+            if n == 0:
+                acts[j] = work3.tile([P, 4 * GW], F32, name="acts")
+            g = psum.tile([P, GW], F32, name="g", tag="bank")
+            sums[(j, n)] = g
+            for s in range(GT):
                 nc.tensor.matmul(
-                    out=g[:], lhsT=h_t_sb[j][:, s * P : (s + 1) * P], rhs=u_t[:], start=False, stop=True
+                    out=g[:, s * HID : (s + 1) * HID],
+                    lhsT=a_sb[j][:, n * GW + s * P : n * GW + (s + 1) * P],
+                    rhs=ident_f[:],
+                    is_transpose=True,
+                    start=(s == 0),
+                    stop=False,
                 )
-                base = s * 4 * HID
-                nc.scalar.activation(out=acts[j][:, base : base + 4 * HID], in_=g[:], func=ACT.Sigmoid)
 
-        def by_tile(ap, tiles):
-            return ap.rearrange("p (t h) -> p t h", t=tiles)
+        def stage_gmm(j, n):
+            g = sums[(j, n)]
+            for s in range(GT):
+                nc.tensor.matmul(
+                    out=g[:, s * HID : (s + 1) * HID],
+                    lhsT=h_t_sb[j][:, s * P : (s + 1) * P],
+                    rhs=u_t[:, n * HID : (n + 1) * HID],
+                    start=False,
+                    stop=(s == GT - 1),
+                )
+            nc.scalar.activation(out=acts[j][:, n * GW : (n + 1) * GW], in_=g[:], func=gate_func[n])
 
-        def gate(j, n, s0, s1):
-            return acts[j][:].rearrange("p (t n h) -> p t n h", t=GT, n=4)[:, s0:s1, n, :]
+        def gate(j, n):
+            return acts[j][:, n * GW : (n + 1) * GW]
 
-        def stage_fc(j, eng, s0, s1):
-            tiles = s1 - s0
-            key = (j, s0)
-            fc[key] = work2.tile([P, tiles * HID], F32, name="fc")
-            eng.tensor_tensor(
-                out=by_tile(fc[key][:], tiles),
-                in0=gate(j, 1, s0, s1),
-                in1=by_tile(c_of[j][:, s0 * HID : s1 * HID], tiles),
-                op=ALU.mult,
-            )
+        def stage_fc(j, eng):
+            fc[j] = work2.tile([P, GW], F32, name="fc")
+            eng.tensor_tensor(out=fc[j][:], in0=gate(j, 0), in1=c_of[j], op=ALU.mult)
 
-        def stage_ic(j, s0, s1):
-            tiles = s1 - s0
-            key = (j, s0)
-            ic[key] = work2.tile([P, tiles * HID], F32, name="ic")
-            nc.vector.scalar_tensor_tensor(
-                out=by_tile(ic[key][:], tiles),
-                in0=gate(j, 3, s0, s1),
-                scalar=-0.5,
-                in1=gate(j, 0, s0, s1),
-                op0=ALU.add,
-                op1=ALU.mult,
-            )
+        def stage_ic(j, eng):
+            ic[j] = work2.tile([P, GW], F32, name="ic")
+            eng.tensor_tensor(out=ic[j][:], in0=gate(j, 1), in1=gate(j, 2), op=ALU.mult)
 
-        def stage_add(j, s0, s1):
-            key = (j, s0)
-            cell[key] = work4.tile([P, (s1 - s0) * HID], F32, name="cell")
-            nc.vector.scalar_tensor_tensor(
-                out=cell[key][:], in0=ic[key][:], scalar=2.0, in1=fc[key][:], op0=ALU.mult, op1=ALU.add
-            )
-            nc.sync.dma_start(out=cell_rows[:, j * GW + s0 * HID : j * GW + s1 * HID], in_=cell[key][:])
+        def stage_add(j):
+            cell[j] = work4.tile([P, GW], F32, name="cell")
+            nc.vector.tensor_tensor(out=cell[j][:], in0=fc[j][:], in1=ic[j][:], op=ALU.add)
+            nc.sync.dma_start(out=cell_rows[:, j * GW : (j + 1) * GW], in_=cell[j][:])
 
-        def stage_tanh(j, s0, s1):
-            key = (j, s0)
-            tanh_c[key] = work2.tile([P, (s1 - s0) * HID], F32, name="tanh_c")
-            nc.scalar.activation(out=tanh_c[key][:], in_=cell[key][:], func=ACT.Tanh)
+        def stage_tanh(j):
+            tanh_c[j] = work2.tile([P, GW], F32, name="tanh_c")
+            nc.scalar.activation(out=tanh_c[j][:], in_=cell[j][:], func=ACT.Tanh)
 
-        def stage_h(j, eng, s0, s1):
-            tiles = s1 - s0
-            nh = work4.tile([P, tiles * HID], F32, name="nh")
-            eng.tensor_tensor(
-                out=by_tile(nh[:], tiles), in0=gate(j, 2, s0, s1), in1=by_tile(tanh_c[(j, s0)][:], tiles), op=ALU.mult
-            )
-            nc.sync.dma_start(out=nh_rows[:, j * GW + s0 * HID : j * GW + s1 * HID], in_=nh[:])
+        def stage_h(j):
+            nh = work4.tile([P, GW], F32, name="nh")
+            nc.vector.tensor_tensor(out=nh[:], in0=gate(j, 3), in1=tanh_c[j][:], op=ALU.mult)
+            nc.sync.dma_start(out=nh_rows[:, j * GW : (j + 1) * GW], in_=nh[:])
 
         on_s = [nc.scalar.copy, nc.scalar.copy]
 
@@ -275,8 +249,7 @@ def tile_lstmcell_t_kernel(
         for n in range(4):
             nc.tensor.transpose(ut[:, n * HID : (n + 1) * HID], u_sb[:, n * HID : (n + 1) * HID], ident_b[:])
         u_t = const.tile([P, 4 * HID], BF16, name="u_t")
-        nc.vector.tensor_copy(out=u_t[:, 0 : 3 * HID], in_=ut[:, 0 : 3 * HID])
-        nc.vector.tensor_scalar_mul(out=u_t[:, 3 * HID : 4 * HID], in0=ut[:, 3 * HID : 4 * HID], scalar1=2.0)
+        nc.vector.tensor_copy(out=u_t[:], in_=ut[:])
         bt = psum.tile([P, P], BF16, name="bt", tag="bank")
         nc.tensor.transpose(bt[:], b_rows[:], ident_b[:])
         bias_col = const.tile([P, 4], F32, name="bias_col")
@@ -285,57 +258,46 @@ def tile_lstmcell_t_kernel(
         stage_q(0)
         stage_tx(1, on_s)
         stage_th(1)
-        stage_mx(0, [0, 2])
+        stage_mx(0, [1, 3])
         stage_q(1)
         stage_tx(2, on_s)
         stage_th(2)
         stage_mx(1, [])
         stage_q(2)
-        for i in range(NG - 2):
+        late = NG - 3
+
+        def product_engine(j):
+            return nc.vector if j >= NG - 2 else nc.gpsimd
+
+        for i in range(NG):
             if i + 3 < NG:
                 stage_tx(i + 3, on_s)
                 stage_th(i + 3)
             if i >= 1:
-                stage_fc(i - 1, nc.gpsimd, 0, GT)
+                stage_ic(i - 1, product_engine(i - 1))
+            if i >= 2:
+                stage_h(i - 2)
+            if i >= 1:
+                stage_add(i - 1)
             if i + 3 < NG:
                 stage_q(i + 3)
-            if i >= 1:
-                stage_ic(i - 1, 0, GT)
-                stage_add(i - 1, 0, GT)
-            if i >= 2:
-                stage_h(i - 2, nc.gpsimd, 0, GT)
-            stage_g(i, 0, GT)
-            if i >= 1:
-                stage_tanh(i - 1, 0, GT)
+            stage_gacc(i, 0)
+            stage_gacc(i, 1)
+            stage_gmm(i, 0)
+            stage_fc(i, product_engine(i))
+            if 1 <= i < late:
+                stage_tanh(i - 1)
             if i + 2 < NG:
                 stage_mx(i + 2, [])
-
-        def cell_on_vector(j, s0, s1):
-            stage_ic(j, s0, s1)
-            stage_fc(j, nc.vector, s0, s1)
-            stage_add(j, s0, s1)
-
-        ga = NG - 3
-        gb = NG - 2
-        gc = NG - 1
-        stage_fc(ga, nc.gpsimd, 0, GT)
-        stage_g(gb, 0, 4)
-        stage_h(ga - 1, nc.vector, 0, GT)
-        stage_ic(ga, 0, GT)
-        cell_on_vector(gb, 0, 2)
-        stage_add(ga, 0, GT)
-        stage_g(gc, 0, 2)
-        stage_tanh(ga, 0, GT)
-        cell_on_vector(gb, 2, 4)
-        stage_tanh(gb, 0, 2)
-        stage_h(ga, nc.vector, 0, GT)
-        stage_g(gc, 2, 4)
-        stage_tanh(gb, 2, 4)
-        stage_h(gb, nc.vector, 0, 2)
-        cell_on_vector(gc, 0, 2)
-        stage_h(gb, nc.vector, 2, 4)
-        stage_tanh(gc, 0, 2)
-        cell_on_vector(gc, 2, 4)
-        stage_h(gc, nc.vector, 0, 2)
-        stage_tanh(gc, 2, 4)
-        stage_h(gc, nc.vector, 2, 4)
+            stage_gmm(i, 1)
+            stage_gacc(i, 2)
+            stage_gmm(i, 2)
+            if i >= late:
+                stage_tanh(i - 1)
+            stage_gacc(i, 3)
+            stage_gmm(i, 3)
+        stage_ic(NG - 1, nc.vector)
+        stage_add(NG - 1)
+        stage_h(NG - 2)
+        stage_tanh(NG - 1)
+        stage_h(NG - 1)

@@ -28,10 +28,9 @@ def tile_lstmcell_t_kernel(
     tc, incoming, old_h, old_c, w_i, b_i, u_i, w_o, b_o, u_o, w_f, b_f, u_f, w_c, b_c, u_c, out_0, out_1
 ):
     nc = tc.nc
-    gate_w = [w_f, w_i, w_c, w_o]
-    gate_u = [u_f, u_i, u_c, u_o]
-    gate_b = [b_f, b_i, b_c, b_o]
-    gate_func = [ACT.Sigmoid, ACT.Sigmoid, ACT.Tanh, ACT.Sigmoid]
+    gate_w = [w_i, w_f, w_o, w_c]
+    gate_u = [u_i, u_f, u_o, u_c]
+    gate_b = [b_i, b_f, b_o, b_c]
 
     x_rows = incoming.rearrange("(p t) k -> p (t k)", t=NT)
     h_rows = old_h.rearrange("(p t) k -> p (t k)", t=NT)
@@ -46,7 +45,6 @@ def tile_lstmcell_t_kernel(
         work3 = ctx.enter_context(tc.tile_pool(name="work3", bufs=3))
         work4 = ctx.enter_context(tc.tile_pool(name="work4", bufs=4))
         psum = ctx.enter_context(tc.psum_pool(name="psum", bufs=8))
-        ctx.enter_context(tc.manual_schedule())
 
         ident_f = const.tile([P, P], F32, name="ident_f")
         make_identity(nc, ident_f[:])
@@ -138,7 +136,6 @@ def tile_lstmcell_t_kernel(
         h_t_sb = {}
         a_sb = {}
         acts = {}
-        sums = {}
         fc = {}
         ic = {}
         cell = {}
@@ -182,57 +179,66 @@ def tile_lstmcell_t_kernel(
                         out=a_sb[j][:, n * GW : (n + 1) * GW], in0=mx[:], scalar1=bias_col[:, n : n + 1]
                     )
 
-        def stage_gacc(j, n):
-            if n == 0:
-                acts[j] = work3.tile([P, 4 * GW], F32, name="acts")
-            g = psum.tile([P, GW], F32, name="g", tag="bank")
-            sums[(j, n)] = g
-            for s in range(GT):
+        def stage_g(j, s0, s1):
+            if s0 == 0:
+                acts[j] = work3.tile([P, GT * 4 * HID], F32, name="acts")
+            for s in range(s0, s1):
+                g = psum.tile([P, 4 * HID], F32, name="g", tag="bank")
+                for n in range(4):
+                    nc.tensor.matmul(
+                        out=g[:, n * HID : (n + 1) * HID],
+                        lhsT=a_sb[j][:, n * GW + s * P : n * GW + (s + 1) * P],
+                        rhs=ident_f[:],
+                        is_transpose=True,
+                        start=(n == 0),
+                        stop=False,
+                    )
                 nc.tensor.matmul(
-                    out=g[:, s * HID : (s + 1) * HID],
-                    lhsT=a_sb[j][:, n * GW + s * P : n * GW + (s + 1) * P],
-                    rhs=ident_f[:],
-                    is_transpose=True,
-                    start=(s == 0),
-                    stop=False,
+                    out=g[:], lhsT=h_t_sb[j][:, s * P : (s + 1) * P], rhs=u_t[:], start=False, stop=True
+                )
+                base = s * 4 * HID
+                nc.scalar.activation(out=acts[j][:, base : base + 3 * HID], in_=g[:, 0 : 3 * HID], func=ACT.Sigmoid)
+                nc.scalar.activation(
+                    out=acts[j][:, base + 3 * HID : base + 4 * HID], in_=g[:, 3 * HID : 4 * HID], func=ACT.Tanh
                 )
 
-        def stage_gmm(j, n):
-            g = sums[(j, n)]
-            for s in range(GT):
-                nc.tensor.matmul(
-                    out=g[:, s * HID : (s + 1) * HID],
-                    lhsT=h_t_sb[j][:, s * P : (s + 1) * P],
-                    rhs=u_t[:, n * HID : (n + 1) * HID],
-                    start=False,
-                    stop=(s == GT - 1),
-                )
-            nc.scalar.activation(out=acts[j][:, n * GW : (n + 1) * GW], in_=g[:], func=gate_func[n])
+        def by_tile(ap, tiles):
+            return ap.rearrange("p (t h) -> p t h", t=tiles)
 
-        def gate(j, n):
-            return acts[j][:, n * GW : (n + 1) * GW]
+        def gate(j, n, s0, s1):
+            return acts[j][:].rearrange("p (t n h) -> p t n h", t=GT, n=4)[:, s0:s1, n, :]
 
-        def stage_fc(j, eng):
-            fc[j] = work2.tile([P, GW], F32, name="fc")
-            eng.tensor_tensor(out=fc[j][:], in0=gate(j, 0), in1=c_of[j], op=ALU.mult)
+        def stage_prod(j, eng, s0, s1):
+            tiles = s1 - s0
+            key = (j, s0)
+            fc[key] = work2.tile([P, tiles * HID], F32, name="fc")
+            ic[key] = work2.tile([P, tiles * HID], F32, name="ic")
+            eng.tensor_tensor(
+                out=by_tile(fc[key][:], tiles),
+                in0=gate(j, 1, s0, s1),
+                in1=by_tile(c_of[j][:, s0 * HID : s1 * HID], tiles),
+                op=ALU.mult,
+            )
+            eng.tensor_tensor(out=by_tile(ic[key][:], tiles), in0=gate(j, 0, s0, s1), in1=gate(j, 3, s0, s1), op=ALU.mult)
 
-        def stage_ic(j, eng):
-            ic[j] = work2.tile([P, GW], F32, name="ic")
-            eng.tensor_tensor(out=ic[j][:], in0=gate(j, 1), in1=gate(j, 2), op=ALU.mult)
+        def stage_add(j, s0, s1):
+            key = (j, s0)
+            cell[key] = work4.tile([P, (s1 - s0) * HID], F32, name="cell")
+            nc.vector.tensor_tensor(out=cell[key][:], in0=fc[key][:], in1=ic[key][:], op=ALU.add)
+            nc.sync.dma_start(out=cell_rows[:, j * GW + s0 * HID : j * GW + s1 * HID], in_=cell[key][:])
 
-        def stage_add(j):
-            cell[j] = work4.tile([P, GW], F32, name="cell")
-            nc.vector.tensor_tensor(out=cell[j][:], in0=fc[j][:], in1=ic[j][:], op=ALU.add)
-            nc.sync.dma_start(out=cell_rows[:, j * GW : (j + 1) * GW], in_=cell[j][:])
+        def stage_tanh(j, s0, s1):
+            key = (j, s0)
+            tanh_c[key] = work2.tile([P, (s1 - s0) * HID], F32, name="tanh_c")
+            nc.scalar.activation(out=tanh_c[key][:], in_=cell[key][:], func=ACT.Tanh)
 
-        def stage_tanh(j):
-            tanh_c[j] = work2.tile([P, GW], F32, name="tanh_c")
-            nc.scalar.activation(out=tanh_c[j][:], in_=cell[j][:], func=ACT.Tanh)
-
-        def stage_h(j):
-            nh = work4.tile([P, GW], F32, name="nh")
-            nc.vector.tensor_tensor(out=nh[:], in0=gate(j, 3), in1=tanh_c[j][:], op=ALU.mult)
-            nc.sync.dma_start(out=nh_rows[:, j * GW : (j + 1) * GW], in_=nh[:])
+        def stage_h(j, s0, s1):
+            tiles = s1 - s0
+            nh = work4.tile([P, tiles * HID], F32, name="nh")
+            nc.vector.tensor_tensor(
+                out=by_tile(nh[:], tiles), in0=gate(j, 2, s0, s1), in1=by_tile(tanh_c[(j, s0)][:], tiles), op=ALU.mult
+            )
+            nc.sync.dma_start(out=nh_rows[:, j * GW + s0 * HID : j * GW + s1 * HID], in_=nh[:])
 
         on_s = [nc.scalar.copy, nc.scalar.copy]
 
@@ -264,40 +270,48 @@ def tile_lstmcell_t_kernel(
         stage_th(2)
         stage_mx(1, [])
         stage_q(2)
-        late = NG - 3
-
-        def product_engine(j):
-            return nc.vector if j >= NG - 2 else nc.gpsimd
-
-        for i in range(NG):
+        for i in range(NG - 2):
             if i + 3 < NG:
                 stage_tx(i + 3, on_s)
                 stage_th(i + 3)
             if i >= 1:
-                stage_ic(i - 1, product_engine(i - 1))
-            if i >= 2:
-                stage_h(i - 2)
-            if i >= 1:
-                stage_add(i - 1)
+                stage_prod(i - 1, nc.gpsimd, 0, GT)
             if i + 3 < NG:
                 stage_q(i + 3)
-            stage_gacc(i, 0)
-            stage_gacc(i, 1)
-            stage_gmm(i, 0)
-            stage_fc(i, product_engine(i))
-            if 1 <= i < late:
-                stage_tanh(i - 1)
+            if i >= 1:
+                stage_add(i - 1, 0, GT)
+            if i >= 2:
+                stage_h(i - 2, 0, GT)
+            stage_g(i, 0, GT)
+            if i >= 1:
+                stage_tanh(i - 1, 0, GT)
             if i + 2 < NG:
                 stage_mx(i + 2, [])
-            stage_gmm(i, 1)
-            stage_gacc(i, 2)
-            stage_gmm(i, 2)
-            if i >= late:
-                stage_tanh(i - 1)
-            stage_gacc(i, 3)
-            stage_gmm(i, 3)
-        stage_ic(NG - 1, nc.vector)
-        stage_add(NG - 1)
-        stage_h(NG - 2)
-        stage_tanh(NG - 1)
-        stage_h(NG - 1)
+
+        ga = NG - 3
+        gb = NG - 2
+        gc = NG - 1
+        stage_prod(ga, nc.gpsimd, 0, GT)
+        stage_g(gb, 0, 4)
+        stage_h(ga - 1, 0, GT)
+        stage_prod(gb, nc.vector, 0, 2)
+        stage_add(gb, 0, 2)
+        stage_add(ga, 0, GT)
+        stage_g(gc, 0, 2)
+        stage_tanh(ga, 0, GT)
+        stage_prod(gb, nc.vector, 2, 4)
+        stage_add(gb, 2, 4)
+        stage_tanh(gb, 0, 2)
+        stage_h(ga, 0, GT)
+        stage_g(gc, 2, 4)
+        stage_tanh(gb, 2, 4)
+        stage_h(gb, 0, 2)
+        stage_prod(gc, nc.vector, 0, 2)
+        stage_add(gc, 0, 2)
+        stage_h(gb, 2, 4)
+        stage_tanh(gc, 0, 2)
+        stage_prod(gc, nc.vector, 2, 4)
+        stage_add(gc, 2, 4)
+        stage_h(gc, 0, 2)
+        stage_tanh(gc, 2, 4)
+        stage_h(gc, 2, 4)

@@ -45,6 +45,7 @@ def tile_lstmcell_t_kernel(
         work3 = ctx.enter_context(tc.tile_pool(name="work3", bufs=3))
         work4 = ctx.enter_context(tc.tile_pool(name="work4", bufs=4))
         psum = ctx.enter_context(tc.psum_pool(name="psum", bufs=8))
+        ctx.enter_context(tc.manual_schedule())
 
         ident_f = const.tile([P, P], F32, name="ident_f")
         make_identity(nc, ident_f[:])
@@ -136,6 +137,7 @@ def tile_lstmcell_t_kernel(
         h_t_sb = {}
         a_sb = {}
         acts = {}
+        sums = {}
         fc = {}
         ic = {}
         cell = {}
@@ -179,28 +181,34 @@ def tile_lstmcell_t_kernel(
                         out=a_sb[j][:, n * GW : (n + 1) * GW], in0=mx[:], scalar1=bias_col[:, n : n + 1]
                     )
 
-        def stage_g(j, s0, s1):
-            if s0 == 0:
-                acts[j] = work3.tile([P, GT * 4 * HID], F32, name="acts")
-            for s in range(s0, s1):
-                g = psum.tile([P, 4 * HID], F32, name="g", tag="bank")
-                for n in range(4):
-                    nc.tensor.matmul(
-                        out=g[:, n * HID : (n + 1) * HID],
-                        lhsT=a_sb[j][:, n * GW + s * P : n * GW + (s + 1) * P],
-                        rhs=ident_f[:],
-                        is_transpose=True,
-                        start=(n == 0),
-                        stop=False,
-                    )
+        def stage_gacc(j, s):
+            if s == 0:
+                acts[j] = work4.tile([P, GT * 4 * HID], F32, name="acts")
+            g = psum.tile([P, 4 * HID], F32, name="g", tag="bank")
+            sums[(j, s)] = g
+            for n in range(4):
                 nc.tensor.matmul(
-                    out=g[:], lhsT=h_t_sb[j][:, s * P : (s + 1) * P], rhs=u_t[:], start=False, stop=True
+                    out=g[:, n * HID : (n + 1) * HID],
+                    lhsT=a_sb[j][:, n * GW + s * P : n * GW + (s + 1) * P],
+                    rhs=ident_f[:],
+                    is_transpose=True,
+                    start=(n == 0),
+                    stop=False,
                 )
-                base = s * 4 * HID
-                nc.scalar.activation(out=acts[j][:, base : base + 3 * HID], in_=g[:, 0 : 3 * HID], func=ACT.Sigmoid)
-                nc.scalar.activation(
-                    out=acts[j][:, base + 3 * HID : base + 4 * HID], in_=g[:, 3 * HID : 4 * HID], func=ACT.Tanh
-                )
+
+        def stage_gmm(j, s):
+            g = sums[(j, s)]
+            nc.tensor.matmul(out=g[:], lhsT=h_t_sb[j][:, s * P : (s + 1) * P], rhs=u_t[:], start=False, stop=True)
+            base = s * 4 * HID
+            nc.scalar.activation(out=acts[j][:, base : base + 3 * HID], in_=g[:, 0 : 3 * HID], func=ACT.Sigmoid)
+            nc.scalar.activation(
+                out=acts[j][:, base + 3 * HID : base + 4 * HID], in_=g[:, 3 * HID : 4 * HID], func=ACT.Tanh
+            )
+
+        def stage_g(j, s0, s1):
+            for s in range(s0, s1):
+                stage_gacc(j, s)
+                stage_gmm(j, s)
 
         def by_tile(ap, tiles):
             return ap.rearrange("p (t h) -> p t h", t=tiles)
@@ -210,21 +218,25 @@ def tile_lstmcell_t_kernel(
 
         def stage_prod(j, eng, s0, s1):
             tiles = s1 - s0
-            key = (j, s0)
-            fc[key] = work2.tile([P, tiles * HID], F32, name="fc")
-            ic[key] = work2.tile([P, tiles * HID], F32, name="ic")
+            if s0 == 0:
+                fc[j] = work2.tile([P, GW], F32, name="fc")
+                ic[j] = work2.tile([P, GW], F32, name="ic")
             eng.tensor_tensor(
-                out=by_tile(fc[key][:], tiles),
+                out=by_tile(fc[j][:, s0 * HID : s1 * HID], tiles),
                 in0=gate(j, 1, s0, s1),
                 in1=by_tile(c_of[j][:, s0 * HID : s1 * HID], tiles),
                 op=ALU.mult,
             )
-            eng.tensor_tensor(out=by_tile(ic[key][:], tiles), in0=gate(j, 0, s0, s1), in1=gate(j, 3, s0, s1), op=ALU.mult)
+            eng.tensor_tensor(
+                out=by_tile(ic[j][:, s0 * HID : s1 * HID], tiles), in0=gate(j, 0, s0, s1), in1=gate(j, 3, s0, s1), op=ALU.mult
+            )
 
         def stage_add(j, s0, s1):
             key = (j, s0)
             cell[key] = work4.tile([P, (s1 - s0) * HID], F32, name="cell")
-            nc.vector.tensor_tensor(out=cell[key][:], in0=fc[key][:], in1=ic[key][:], op=ALU.add)
+            nc.vector.tensor_tensor(
+                out=cell[key][:], in0=fc[j][:, s0 * HID : s1 * HID], in1=ic[j][:, s0 * HID : s1 * HID], op=ALU.add
+            )
             nc.sync.dma_start(out=cell_rows[:, j * GW + s0 * HID : j * GW + s1 * HID], in_=cell[key][:])
 
         def stage_tanh(j, s0, s1):
@@ -275,23 +287,28 @@ def tile_lstmcell_t_kernel(
                 stage_tx(i + 3, on_s)
                 stage_th(i + 3)
             if i >= 1:
-                stage_prod(i - 1, nc.gpsimd, 0, GT)
+                stage_prod(i - 1, nc.gpsimd, 2, 4)
             if i + 3 < NG:
                 stage_q(i + 3)
             if i >= 1:
                 stage_add(i - 1, 0, GT)
             if i >= 2:
                 stage_h(i - 2, 0, GT)
-            stage_g(i, 0, GT)
+            stage_g(i, 0, 2)
+            stage_prod(i, nc.gpsimd, 0, 2)
+            stage_gacc(i, 2)
+            stage_gacc(i, 3)
+            stage_gmm(i, 2)
             if i >= 1:
                 stage_tanh(i - 1, 0, GT)
             if i + 2 < NG:
                 stage_mx(i + 2, [])
+            stage_gmm(i, 3)
 
         ga = NG - 3
         gb = NG - 2
         gc = NG - 1
-        stage_prod(ga, nc.gpsimd, 0, GT)
+        stage_prod(ga, nc.gpsimd, 2, 4)
         stage_g(gb, 0, 4)
         stage_h(ga - 1, 0, GT)
         stage_prod(gb, nc.vector, 0, 2)

from contextlib import ExitStack

import concourse.mybir as mybir
from concourse.masks import make_identity

F32 = mybir.dt.float32
BF16 = mybir.dt.bfloat16
U32 = mybir.dt.uint32
U8 = mybir.dt.uint8
FP8X4 = mybir.dt.float8_e4m3fn_x4
ACT = mybir.ActivationFunctionType
ALU = mybir.AluOpType

P = 128
BATCH = 8192
IN_F = 512
HID = 128
NT = BATCH // P
GT = 4
NG = NT // GT
GW = GT * P
HC_SIZES = [2, 2, 4, 4, 4]

FLOPS = 2 * BATCH * (IN_F + HID) * 4 * HID


def tile_lstmcell_t_kernel(
    tc, incoming, old_h, old_c, w_i, b_i, u_i, w_o, b_o, u_o, w_f, b_f, u_f, w_c, b_c, u_c, out_0, out_1
):
    nc = tc.nc
    gate_w = [w_i, w_f, w_o, w_c]
    gate_u = [u_i, u_f, u_o, u_c]
    gate_b = [b_i, b_f, b_o, b_c]

    x_rows = incoming.rearrange("(p t) k -> p (t k)", t=NT)
    h_rows = old_h.rearrange("(p t) k -> p (t k)", t=NT)
    c_rows = old_c.rearrange("(p t) k -> p (t k)", t=NT)
    nh_rows = out_0.rearrange("(p t) k -> p (t k)", t=NT)
    cell_rows = out_1.rearrange("(p t) k -> p (t k)", t=NT)

    with ExitStack() as ctx:
        const = ctx.enter_context(tc.tile_pool(name="const", bufs=1))
        resident = ctx.enter_context(tc.tile_pool(name="resident", bufs=1))
        work2 = ctx.enter_context(tc.tile_pool(name="work2", bufs=2))
        work3 = ctx.enter_context(tc.tile_pool(name="work3", bufs=3))
        work4 = ctx.enter_context(tc.tile_pool(name="work4", bufs=4))
        psum = ctx.enter_context(tc.psum_pool(name="psum", bufs=8))
        ctx.enter_context(tc.manual_schedule())

        ident_f = const.tile([P, P], F32, name="ident_f")
        make_identity(nc, ident_f[:])
        ident_b = const.tile([P, P], BF16, name="ident_b")
        make_identity(nc, ident_b[:])

        warm = const.tile([P, 1], F32, name="warm")
        nc.vector.memset(warm[:], 0.0)
        warm_out = const.tile([P, 1], F32, name="warm_out")
        nc.scalar.activation(out=warm_out[:], in_=warm[:], func=ACT.Sigmoid)

        x_sb = {}
        h_of = {}
        c_of = {}

        def load_x(j):
            x_sb[j] = resident.tile([P, GT * IN_F], BF16, name="x%d" % j)
            nc.sync.dma_start(out=x_sb[j][:], in_=x_rows[:, j * GT * IN_F : (j + 1) * GT * IN_F])

        def load_hc(m, rows, table, letter):
            first = sum(HC_SIZES[:m])
            t = resident.tile([P, HC_SIZES[m] * GW], BF16, name="%s%d" % (letter, m))
            nc.sync.dma_start(out=t[:], in_=rows[:, first * GW : (first + HC_SIZES[m]) * GW])
            for r in range(HC_SIZES[m]):
                table[first + r] = t[:, r * GW : (r + 1) * GW]

        def load_h(m):
            load_hc(m, h_rows, h_of, "h")

        def load_c(m):
            load_hc(m, c_rows, c_of, "c")

        w_sb = const.tile([P, 4 * IN_F], BF16, name="w_sb")
        for n in range(4):
            nc.sync.dma_start(out=w_sb[:, n * IN_F : (n + 1) * IN_F], in_=gate_w[n])
        load_x(0)
        load_h(0)
        u_sb = const.tile([P, 4 * HID], BF16, name="u_sb")
        for n in range(4):
            nc.scalar.dma_start(out=u_sb[:, n * HID : (n + 1) * HID], in_=gate_u[n])
        b_rows = const.tile([P, P], BF16, name="b_rows")
        nc.vector.memset(b_rows[:], 0.0)
        for n in range(4):
            nc.scalar.dma_start(out=b_rows[n : n + 1, :], in_=gate_b[n].rearrange("(o h) -> o h", o=1))
        load_x(1)
        load_x(2)
        load_c(0)
        load_h(1)
        load_x(3)
        load_c(1)
        load_x(4)
        load_h(2)
        load_x(5)
        load_c(2)
        load_x(6)
        load_x(7)
        load_x(8)
        load_h(3)
        load_c(3)
        load_x(9)
        load_x(10)
        load_x(11)
        load_x(12)
        load_h(4)
        load_c(4)
        load_x(13)
        load_x(14)
        load_x(15)

        def transpose_words(src, grouped, copies):
            words = src[:].bitcast(F32)
            out_words = grouped[:].bitcast(F32).rearrange("q (s c u) -> q s c u", s=4, u=2)
            for half in range(2):
                bank = psum.tile([P, 512], F32, name="bank", tag="bank")
                for s in range(2):
                    for u in range(2):
                        first = (2 * half + s) * 256 + u * P
                        nc.tensor.transpose(
                            bank[:, (2 * s + u) * P : (2 * s + u + 1) * P], words[:, first : first + P], ident_f[:]
                        )
                copies[half](
                    out=out_words[:, 2 * half : 2 * half + 2],
                    in_=bank[:].rearrange("q (s u c) -> q s c u", s=2, u=2),
                )

        grouped = {}
        codes = {}
        scales = {}
        h_t_sb = {}
        a_sb = {}
        acts = {}
        sums = {}
        fc = {}
        ic = {}
        cell = {}
        tanh_c = {}

        def stage_tx(j, copies):
            grouped[j] = work2.tile([P, GW * 4], BF16, name="grouped", align_bytes=64)
            transpose_words(x_sb[j], grouped[j], copies)

        def stage_th(j):
            ht = psum.tile([P, GW], BF16, name="ht", tag="bank")
            for s in range(GT):
                nc.tensor.transpose(ht[:, s * P : (s + 1) * P], h_of[j][:, s * P : (s + 1) * P], ident_b[:])
            h_t_sb[j] = work4.tile([P, GW], BF16, name="h_t_sb")
            nc.vector.tensor_copy(out=h_t_sb[j][:], in_=ht[:])

        def stage_q(j):
            codes[j] = work3.tile([P, GW], U32, name="codes", align_bytes=64)
            scales[j] = work3.tile([P, GW], U8, name="scales", align_bytes=64)
            nc.vector.quantize_mx(out=codes[j][:].bitcast(FP8X4), scales=scales[j][:], in_=grouped[j][:])

        def stage_mx(j, on_scalar):
            a_sb[j] = work3.tile([P, 4 * GW], F32, name="a_sb")
            for n in range(4):
                mx = psum.tile([P, GW], F32, name="mx", tag="bank")
                nc.tensor.matmul_mx(
                    out=mx[:],
                    lhsT=w_codes[:, n * P : (n + 1) * P].bitcast(FP8X4),
                    lhsT_scale=w_scales[:, n * P : (n + 1) * P],
                    rhs=codes[j][:].bitcast(FP8X4),
                    rhs_scale=scales[j][:],
                    start=True,
                    stop=True,
                )
                if n in on_scalar:
                    nc.scalar.activation(
                        out=a_sb[j][:, n * GW : (n + 1) * GW], in_=mx[:], func=ACT.Identity, bias=bias_col[:, n : n + 1]
                    )
                else:
                    nc.vector.tensor_scalar_add(
                        out=a_sb[j][:, n * GW : (n + 1) * GW], in0=mx[:], scalar1=bias_col[:, n : n + 1]
                    )

        def stage_gacc(j, s):
            if s == 0:
                acts[j] = work4.tile([P, GT * 4 * HID], F32, name="acts")
            g = psum.tile([P, 4 * HID], F32, name="g", tag="bank")
            sums[(j, s)] = g
            for n in range(4):
                nc.tensor.matmul(
                    out=g[:, n * HID : (n + 1) * HID],
                    lhsT=a_sb[j][:, n * GW + s * P : n * GW + (s + 1) * P],
                    rhs=ident_f[:],
                    is_transpose=True,
                    start=(n == 0),
                    stop=False,
                )

        def stage_gmm(j, s):
            g = sums[(j, s)]
            nc.tensor.matmul(out=g[:], lhsT=h_t_sb[j][:, s * P : (s + 1) * P], rhs=u_t[:], start=False, stop=True)
            base = s * 4 * HID
            nc.scalar.activation(out=acts[j][:, base : base + 3 * HID], in_=g[:, 0 : 3 * HID], func=ACT.Sigmoid)
            nc.scalar.activation(
                out=acts[j][:, base + 3 * HID : base + 4 * HID], in_=g[:, 3 * HID : 4 * HID], func=ACT.Tanh
            )

        def stage_g(j, s0, s1):
            for s in range(s0, s1):
                stage_gacc(j, s)
                stage_gmm(j, s)

        def by_tile(ap, tiles):
            return ap.rearrange("p (t h) -> p t h", t=tiles)

        def gate(j, n, s0, s1):
            return acts[j][:].rearrange("p (t n h) -> p t n h", t=GT, n=4)[:, s0:s1, n, :]

        def stage_prod(j, eng, s0, s1):
            tiles = s1 - s0
            if s0 == 0:
                fc[j] = work2.tile([P, GW], F32, name="fc")
                ic[j] = work2.tile([P, GW], F32, name="ic")
            eng.tensor_tensor(
                out=by_tile(fc[j][:, s0 * HID : s1 * HID], tiles),
                in0=gate(j, 1, s0, s1),
                in1=by_tile(c_of[j][:, s0 * HID : s1 * HID], tiles),
                op=ALU.mult,
            )
            eng.tensor_tensor(
                out=by_tile(ic[j][:, s0 * HID : s1 * HID], tiles), in0=gate(j, 0, s0, s1), in1=gate(j, 3, s0, s1), op=ALU.mult
            )

        def stage_add(j, s0, s1):
            key = (j, s0)
            cell[key] = work4.tile([P, (s1 - s0) * HID], F32, name="cell")
            nc.vector.tensor_tensor(
                out=cell[key][:], in0=fc[j][:, s0 * HID : s1 * HID], in1=ic[j][:, s0 * HID : s1 * HID], op=ALU.add
            )
            nc.sync.dma_start(out=cell_rows[:, j * GW + s0 * HID : j * GW + s1 * HID], in_=cell[key][:])

        def stage_tanh(j, s0, s1):
            key = (j, s0)
            tanh_c[key] = work2.tile([P, (s1 - s0) * HID], F32, name="tanh_c")
            nc.scalar.activation(out=tanh_c[key][:], in_=cell[key][:], func=ACT.Tanh)

        def stage_h(j, s0, s1):
            tiles = s1 - s0
            nh = work4.tile([P, tiles * HID], F32, name="nh")
            nc.vector.tensor_tensor(
                out=by_tile(nh[:], tiles), in0=gate(j, 2, s0, s1), in1=by_tile(tanh_c[(j, s0)][:], tiles), op=ALU.mult
            )
            nc.sync.dma_start(out=nh_rows[:, j * GW + s0 * HID : j * GW + s1 * HID], in_=nh[:])

        on_s = [nc.scalar.copy, nc.scalar.copy]

        w_grouped = const.tile([P, 4 * P * 4], BF16, name="w_grouped", align_bytes=64)
        transpose_words(w_sb, w_grouped, [nc.vector.tensor_copy, nc.vector.tensor_copy])
        w_codes = const.tile([P, 4 * P], U32, name="w_codes", align_bytes=64)
        w_scales = const.tile([P, 4 * P], U8, name="w_scales", align_bytes=64)
        nc.vector.quantize_mx(out=w_codes[:].bitcast(FP8X4), scales=w_scales[:], in_=w_grouped[:])

        stage_tx(0, [nc.scalar.copy, nc.vector.tensor_copy])
        stage_th(0)

        ut = psum.tile([P, 4 * HID], BF16, name="ut", tag="bank")
        for n in range(4):
            nc.tensor.transpose(ut[:, n * HID : (n + 1) * HID], u_sb[:, n * HID : (n + 1) * HID], ident_b[:])
        u_t = const.tile([P, 4 * HID], BF16, name="u_t")
        nc.vector.tensor_copy(out=u_t[:], in_=ut[:])
        bt = psum.tile([P, P], BF16, name="bt", tag="bank")
        nc.tensor.transpose(bt[:], b_rows[:], ident_b[:])
        bias_col = const.tile([P, 4], F32, name="bias_col")
        nc.vector.tensor_copy(out=bias_col[:], in_=bt[:, 0:4])

        stage_q(0)
        stage_tx(1, on_s)
        stage_th(1)
        stage_mx(0, [1, 3])
        stage_q(1)
        stage_tx(2, on_s)
        stage_th(2)
        stage_mx(1, [])
        stage_q(2)
        for i in range(NG - 2):
            if i + 3 < NG:
                stage_tx(i + 3, on_s)
                stage_th(i + 3)
            if i >= 1:
                stage_prod(i - 1, nc.gpsimd, 2, 4)
            if i + 3 < NG:
                stage_q(i + 3)
            if i >= 1:
                stage_add(i - 1, 0, GT)
            if i >= 2:
                stage_h(i - 2, 0, GT)
            stage_g(i, 0, 2)
            stage_prod(i, nc.gpsimd, 0, 2)
            stage_gacc(i, 2)
            stage_gacc(i, 3)
            stage_gmm(i, 2)
            if i >= 1:
                stage_tanh(i - 1, 0, GT)
            if i + 2 < NG:
                stage_mx(i + 2, [])
            stage_gmm(i, 3)

        ga = NG - 3
        gb = NG - 2
        gc = NG - 1
        stage_prod(ga, nc.gpsimd, 2, 4)
        stage_g(gb, 0, 4)
        stage_h(ga - 1, 0, GT)
        stage_prod(gb, nc.vector, 0, 2)
        stage_add(gb, 0, 2)
        stage_add(ga, 0, GT)
        stage_g(gc, 0, 2)
        stage_tanh(ga, 0, GT)
        stage_prod(gb, nc.vector, 2, 4)
        stage_add(gb, 2, 4)
        stage_tanh(gb, 0, 2)
        stage_h(ga, 0, GT)
        stage_g(gc, 2, 4)
        stage_tanh(gb, 2, 4)
        stage_h(gb, 0, 2)
        stage_prod(gc, nc.vector, 0, 2)
        stage_add(gc, 0, 2)
        stage_h(gb, 2, 4)
        stage_tanh(gc, 0, 2)
        stage_prod(gc, nc.vector, 2, 4)
        stage_add(gc, 2, 4)
        stage_h(gc, 0, 2)
        stage_tanh(gc, 2, 4)
        stage_h(gc, 2, 4)
